import numpy as np
import ml_dtypes

BF16 = ml_dtypes.bfloat16


def bf(x):
    return np.asarray(x, np.float32).astype(BF16)


def f32(x):
    return np.asarray(x, np.float32)


def f64(x):
    return np.asarray(x).astype(np.float64)


def striped(idx):
    return np.tile(idx.reshape(-1, 16).T, (8, 1))


D, S, F, M, N = 128, 4096, 128, 256, 2048
ALPHA = 1.702
LIMIT = 7.0


def setup_inputs():
    return {"x": bf(np.random.standard_normal((D, S))), "w1": bf(3.0 * np.random.standard_normal((D, M)) / np.sqrt(D)), "b1": f32(0.3 * np.random.standard_normal((M, 1))), "w2": bf(0.25 * np.random.standard_normal((F, D)) / np.sqrt(F)), "b2": f32(0.2 * np.random.standard_normal((D, 1))), "ew": f32(0.1 + 0.9 * np.random.random_sample((1, N))), "offs": striped(np.random.permutation(S)[:N])}


def reference(x, w1, b1, w2, b2, ew, offs):
    idx = offs[:16].T.reshape(-1)
    t = f64(w1).T @ f64(x)[:, idx] + f64(b1)
    glu = np.minimum(t[:F], LIMIT)
    lin = np.maximum(np.minimum(t[F:], LIMIT), -LIMIT)
    h = glu / (1.0 + np.exp(-ALPHA * glu)) * (lin + 1.0)
    return (f64(w2).T @ h + f64(b2)) * f64(ew)

@@ -1,0 +1,95 @@
+import concourse.mybir as mybir
+
+P = 128
+TOKENS = 4096
+ROUTED = 2048
+PIECE = 512
+PIECES = ROUTED // PIECE
+OFFSET_COLUMNS = PIECE // 16
+PSUM_BANKS = 8
+LIMIT = 7.0
+
+FLOPS = 2 * P * (2 * P) * ROUTED + 2 * P * P * ROUTED
+
+BF16, F32, U16 = mybir.dt.bfloat16, mybir.dt.float32, mybir.dt.uint16
+ADD, MULT = mybir.AluOpType.add, mybir.AluOpType.mult
+MIN, MAX = mybir.AluOpType.min, mybir.AluOpType.max
+SWISH = mybir.ActivationFunctionType.Gelu_apprx_sigmoid
+IDENTITY = mybir.ActivationFunctionType.Identity
+
+
+def tile_moemlpfused_kernel(tc, x, w1, b1, w2, b2, ew, offs, out):
+    nc = tc.nc
+    with (
+        tc.tile_pool(name="held", bufs=1) as held,
+        tc.tile_pool(name="work", bufs=PIECES) as work,
+        tc.psum_pool(name="psum", bufs=1) as psum,
+    ):
+        offsets = held.tile([P, ROUTED // 16], U16, name="offsets")
+        tokens = held.tile([P, TOKENS], BF16, name="tokens")
+        w1_sb = held.tile([P, 2 * P], BF16, name="w1_sb")
+        w2_sb = held.tile([P, P], BF16, name="w2_sb")
+        b1_sb = held.tile([P, 2], F32, name="b1_sb")
+        b1_lin1 = held.tile([P, 1], F32, name="b1_lin1")
+        b2_sb = held.tile([P, 1], F32, name="b2_sb")
+        routing = held.tile([P, ROUTED], F32, name="routing")
+        limit = held.tile([P, 1], F32, name="limit")
+        swish_cap = held.tile([P, 1], F32, name="swish_cap")
+        banks = [psum.tile([P, PIECE], F32, name=f"bank{b}") for b in range(PSUM_BANKS)]
+
+        nc.scalar.dma_start(tokens[:], x)
+        nc.sync.dma_start(offsets[:], offs)
+        nc.sync.dma_start(w1_sb[:], w1)
+        nc.scalar.dma_start(b1_sb[:], b1.rearrange("(half p) one -> p (half one)", p=P))
+        nc.scalar.dma_start(w2_sb[:], w2)
+        nc.scalar.dma_start(b2_sb[:], b2)
+        nc.scalar.dma_start(routing[:], ew.broadcast_to([P, ROUTED]))
+
+        nc.vector.memset(limit[:], LIMIT)
+        nc.scalar.activation(swish_cap[:], limit[:], SWISH)
+
+        nc.vector.tensor_scalar_add(b1_lin1[:], b1_sb[:, 1:2], 1.0)
+
+        for piece in range(PIECES):
+            picked = tokens[:].indirect(
+                offsets[:, piece * OFFSET_COLUMNS : (piece + 1) * OFFSET_COLUMNS]
+            )
+            nc.tensor.matmul(banks[2 * piece][:], w1_sb[:, P : 2 * P], picked)
+            nc.tensor.matmul(banks[2 * piece + 1][:], w1_sb[:, 0:P], picked)
+
+        h = []
+        for piece in range(PIECES):
+            t_lin, t_gate = banks[2 * piece], banks[2 * piece + 1]
+            lin_raw = work.tile([P, PIECE], F32, name="lin_raw")
+            nc.scalar.activation(lin_raw[:], t_lin[:], IDENTITY, bias=b1_lin1[:])
+            lin1 = work.tile([P, PIECE], F32, name="lin1")
+            nc.vector.tensor_scalar(
+                lin1[:], lin_raw[:], LIMIT + 1.0, -LIMIT + 1.0, MIN, MAX
+            )
+            swish = work.tile([P, PIECE], F32, name="swish")
+            h.append(work.tile([P, PIECE], BF16, name="h"))
+            parts = 2 if piece == PIECES - 1 else 1
+            width = PIECE // parts
+            for part in range(parts):
+                local = slice(part * width, (part + 1) * width)
+                nc.scalar.activation(
+                    swish[:, local], t_gate[:, local], SWISH, bias=b1_sb[:, 0:1]
+                )
+                nc.vector.scalar_tensor_tensor(
+                    h[piece][:, local], swish[:, local], swish_cap[:], lin1[:, local], MIN, MULT
+                )
+
+        for piece in range(PIECES):
+            y = banks[2 * (PIECES - 1 - piece // 2) + piece % 2]
+            nc.tensor.matmul(y[:], w2_sb[:], h[piece][:])
+            scaled = work.tile([P, PIECE], F32, name="scaled")
+            parts = 2 if piece == PIECES - 1 else 1
+            width = PIECE // parts
+            for part in range(parts):
+                local = slice(part * width, (part + 1) * width)
+                columns = slice(piece * PIECE + part * width, piece * PIECE + (part + 1) * width)
+                nc.vector.scalar_tensor_tensor(
+                    scaled[:, local], y[:, local], b2_sb[:], routing[:, columns], ADD, MULT
+                )
+                store_queue = nc.sync if (piece + part) % 2 == 0 else nc.scalar
+                store_queue.dma_start(out[:, columns], scaled[:, local])

@@ -50,46 +50,72 @@ def tile_moemlpfused_kernel(tc, x, w1, b1, w2, b2, ew, offs, out):
 
         nc.vector.tensor_scalar_add(b1_lin1[:], b1_sb[:, 1:2], 1.0)
 
-        for piece in range(PIECES):
-            picked = tokens[:].indirect(
-                offsets[:, piece * OFFSET_COLUMNS : (piece + 1) * OFFSET_COLUMNS]
-            )
-            nc.tensor.matmul(banks[2 * piece][:], w1_sb[:, P : 2 * P], picked)
-            nc.tensor.matmul(banks[2 * piece + 1][:], w1_sb[:, 0:P], picked)
+        last = PIECES - 1
+        halves = [slice(0, PIECE // 2), slice(PIECE // 2, PIECE)]
+        lin_bank = [banks[2 * piece] for piece in range(PIECES)]
+        gate_bank = [banks[2 * piece + 1] for piece in range(PIECES)]
+        last_gate_bank = [gate_bank[last], lin_bank[0]]
 
-        h = []
-        for piece in range(PIECES):
-            t_lin, t_gate = banks[2 * piece], banks[2 * piece + 1]
+        def gather(bank, half_of_w1, piece, local):
+            first = piece * PIECE + local.start
+            picked = tokens[:].indirect(offsets[:, first // 16 : (piece * PIECE + local.stop) // 16])
+            nc.tensor.matmul(bank[:, local], w1_sb[:, half_of_w1 * P : (half_of_w1 + 1) * P], picked)
+
+        whole = slice(0, PIECE)
+        swish = [work.tile([P, PIECE], F32, name="swish") for _ in range(PIECES)]
+        lin1 = [work.tile([P, PIECE], F32, name="lin1") for _ in range(PIECES)]
+        h = [work.tile([P, PIECE], BF16, name="h") for _ in range(PIECES)]
+        scaled = [work.tile([P, PIECE], F32, name="scaled") for _ in range(PIECES)]
+
+        def linear_half(piece):
             lin_raw = work.tile([P, PIECE], F32, name="lin_raw")
-            nc.scalar.activation(lin_raw[:], t_lin[:], IDENTITY, bias=b1_lin1[:])
-            lin1 = work.tile([P, PIECE], F32, name="lin1")
+            nc.scalar.activation(lin_raw[:], lin_bank[piece][:], IDENTITY, bias=b1_lin1[:])
             nc.vector.tensor_scalar(
-                lin1[:], lin_raw[:], LIMIT + 1.0, -LIMIT + 1.0, MIN, MAX
+                lin1[piece][:], lin_raw[:], LIMIT + 1.0, -LIMIT + 1.0, MIN, MAX
             )
-            swish = work.tile([P, PIECE], F32, name="swish")
-            h.append(work.tile([P, PIECE], BF16, name="h"))
-            parts = 2 if piece == PIECES - 1 else 1
-            width = PIECE // parts
-            for part in range(parts):
-                local = slice(part * width, (part + 1) * width)
-                nc.scalar.activation(
-                    swish[:, local], t_gate[:, local], SWISH, bias=b1_sb[:, 0:1]
-                )
-                nc.vector.scalar_tensor_tensor(
-                    h[piece][:, local], swish[:, local], swish_cap[:], lin1[:, local], MIN, MULT
-                )
 
-        for piece in range(PIECES):
-            y = banks[2 * (PIECES - 1 - piece // 2) + piece % 2]
-            nc.tensor.matmul(y[:], w2_sb[:], h[piece][:])
-            scaled = work.tile([P, PIECE], F32, name="scaled")
-            parts = 2 if piece == PIECES - 1 else 1
-            width = PIECE // parts
-            for part in range(parts):
-                local = slice(part * width, (part + 1) * width)
-                columns = slice(piece * PIECE + part * width, piece * PIECE + (part + 1) * width)
-                nc.vector.scalar_tensor_tensor(
-                    scaled[:, local], y[:, local], b2_sb[:], routing[:, columns], ADD, MULT
-                )
-                store_queue = nc.sync if (piece + part) % 2 == 0 else nc.scalar
-                store_queue.dma_start(out[:, columns], scaled[:, local])
+        def gate_and_product(bank, piece, local):
+            nc.scalar.activation(swish[piece][:, local], bank[:, local], SWISH, bias=b1_sb[:, 0:1])
+            nc.vector.scalar_tensor_tensor(
+                h[piece][:, local], swish[piece][:, local], swish_cap[:], lin1[piece][:, local], MIN, MULT
+            )
+
+        def project(y, piece, local):
+            nc.tensor.matmul(y[:, local], w2_sb[:], h[piece][:, local])
+
+        def scale_and_store(y, piece, local, queue):
+            columns = slice(piece * PIECE + local.start, piece * PIECE + local.stop)
+            nc.vector.scalar_tensor_tensor(
+                scaled[piece][:, local], y[:, local], b2_sb[:], routing[:, columns], ADD, MULT
+            )
+            queue.dma_start(out[:, columns], scaled[piece][:, local])
+
+        for piece in range(last):
+            gather(lin_bank[piece], 1, piece, whole)
+            gather(gate_bank[piece], 0, piece, whole)
+        gather(lin_bank[last], 1, last, whole)
+        gather(last_gate_bank[0], 0, last, halves[0])
+        linear_half(0)
+        gather(last_gate_bank[1], 0, last, halves[1])
+
+        for piece in range(last):
+            gate_and_product(gate_bank[piece], piece, whole)
+            linear_half(piece + 1)
+
+        gate_and_product(last_gate_bank[0], last, halves[0])
+        y = lin_bank[last]
+        for local in halves:
+            project(y, 0, local)
+        scale_and_store(y, 0, halves[0], nc.sync)
+        gate_and_product(last_gate_bank[1], last, halves[1])
+        scale_and_store(y, 0, halves[1], nc.sync)
+        y = last_gate_bank[0]
+        project(y, 1, whole)
+        scale_and_store(y, 1, whole, nc.scalar)
+        y = last_gate_bank[1]
+        project(y, 2, whole)
+        scale_and_store(y, 2, whole, nc.sync)
+        y = lin_bank[last - 1]
+        project(y, last, whole)
+        scale_and_store(y, last, halves[0], nc.scalar)
+        scale_and_store(y, last, halves[1], nc.sync)

@@ -111,11 +111,16 @@ def tile_moemlpfused_kernel(tc, x, w1, b1, w2, b2, ew, offs, out):
         scale_and_store(y, 0, halves[1], nc.sync)
         y = last_gate_bank[0]
         project(y, 1, whole)
-        scale_and_store(y, 1, whole, nc.scalar)
+        for local in halves:
+            columns = slice(PIECE + local.start, PIECE + local.stop)
+            shifted = work.tile([P, PIECE // 2], F32, name="shifted")
+            nc.scalar.activation(shifted[:], y[:, local], IDENTITY, bias=b2_sb[:])
+            nc.gpsimd.tensor_tensor(scaled[1][:, local], shifted[:], routing[:, columns], MULT)
+            nc.scalar.dma_start(out[:, columns], scaled[1][:, local])
         y = last_gate_bank[1]
         project(y, 2, whole)
         scale_and_store(y, 2, whole, nc.sync)
         y = lin_bank[last - 1]
         project(y, last, whole)
-        scale_and_store(y, last, halves[0], nc.scalar)
+        scale_and_store(y, last, halves[0], nc.sync)
         scale_and_store(y, last, halves[1], nc.sync)

@@ -111,12 +111,12 @@ def tile_moemlpfused_kernel(tc, x, w1, b1, w2, b2, ew, offs, out):
         scale_and_store(y, 0, halves[1], nc.sync)
         y = last_gate_bank[0]
         project(y, 1, whole)
-        for local in halves:
-            columns = slice(PIECE + local.start, PIECE + local.stop)
-            shifted = work.tile([P, PIECE // 2], F32, name="shifted")
-            nc.scalar.activation(shifted[:], y[:, local], IDENTITY, bias=b2_sb[:])
-            nc.gpsimd.tensor_tensor(scaled[1][:, local], shifted[:], routing[:, columns], MULT)
-            nc.scalar.dma_start(out[:, columns], scaled[1][:, local])
+        columns = slice(PIECE, PIECE + PIECE // 2)
+        shifted = work.tile([P, PIECE // 2], F32, name="shifted")
+        nc.scalar.activation(shifted[:], y[:, halves[0]], IDENTITY, bias=b2_sb[:])
+        nc.gpsimd.tensor_tensor(scaled[1][:, halves[0]], shifted[:], routing[:, columns], MULT)
+        nc.scalar.dma_start(out[:, columns], scaled[1][:, halves[0]])
+        scale_and_store(y, 1, halves[1], nc.sync)
         y = last_gate_bank[1]
         project(y, 2, whole)
         scale_and_store(y, 2, whole, nc.sync)

@@ -50,22 +50,17 @@ def tile_moemlpfused_kernel(tc, x, w1, b1, w2, b2, ew, offs, out):
 
         nc.vector.tensor_scalar_add(b1_lin1[:], b1_sb[:, 1:2], 1.0)
 
-        last = PIECES - 1
-        halves = [slice(0, PIECE // 2), slice(PIECE // 2, PIECE)]
         lin_bank = [banks[2 * piece] for piece in range(PIECES)]
         gate_bank = [banks[2 * piece + 1] for piece in range(PIECES)]
-        last_gate_bank = [gate_bank[last], lin_bank[0]]
+        for piece in range(PIECES):
+            picked = tokens[:].indirect(
+                offsets[:, piece * OFFSET_COLUMNS : (piece + 1) * OFFSET_COLUMNS]
+            )
+            nc.tensor.matmul(lin_bank[piece][:], w1_sb[:, P : 2 * P], picked)
+            nc.tensor.matmul(gate_bank[piece][:], w1_sb[:, 0:P], picked)
 
-        def gather(bank, half_of_w1, piece, local):
-            first = piece * PIECE + local.start
-            picked = tokens[:].indirect(offsets[:, first // 16 : (piece * PIECE + local.stop) // 16])
-            nc.tensor.matmul(bank[:, local], w1_sb[:, half_of_w1 * P : (half_of_w1 + 1) * P], picked)
-
-        whole = slice(0, PIECE)
-        swish = [work.tile([P, PIECE], F32, name="swish") for _ in range(PIECES)]
-        lin1 = [work.tile([P, PIECE], F32, name="lin1") for _ in range(PIECES)]
         h = [work.tile([P, PIECE], BF16, name="h") for _ in range(PIECES)]
-        scaled = [work.tile([P, PIECE], F32, name="scaled") for _ in range(PIECES)]
+        lin1 = [work.tile([P, PIECE], F32, name="lin1") for _ in range(PIECES)]
 
         def linear_half(piece):
             lin_raw = work.tile([P, PIECE], F32, name="lin_raw")
@@ -74,53 +69,49 @@ def tile_moemlpfused_kernel(tc, x, w1, b1, w2, b2, ew, offs, out):
                 lin1[piece][:], lin_raw[:], LIMIT + 1.0, -LIMIT + 1.0, MIN, MAX
             )
 
-        def gate_and_product(bank, piece, local):
-            nc.scalar.activation(swish[piece][:, local], bank[:, local], SWISH, bias=b1_sb[:, 0:1])
+        def gate_and_product(piece):
+            swish = work.tile([P, PIECE], F32, name="swish")
+            nc.scalar.activation(swish[:], gate_bank[piece][:], SWISH, bias=b1_sb[:, 0:1])
             nc.vector.scalar_tensor_tensor(
-                h[piece][:, local], swish[piece][:, local], swish_cap[:], lin1[piece][:, local], MIN, MULT
+                h[piece][:], swish[:], swish_cap[:], lin1[piece][:], MIN, MULT
             )
 
-        def project(y, piece, local):
-            nc.tensor.matmul(y[:, local], w2_sb[:], h[piece][:, local])
+        last = PIECES - 1
+        y_bank = [gate_bank[last - 1], lin_bank[last], gate_bank[last], lin_bank[last - 1]]
 
-        def scale_and_store(y, piece, local, queue):
+        def project(piece):
+            nc.tensor.matmul(y_bank[piece][:], w2_sb[:], h[piece][:])
+
+        HALF = PIECE // 2
+
+        def scale_and_store(piece, half, by_gpsimd=False):
+            local = slice(half * HALF, (half + 1) * HALF)
             columns = slice(piece * PIECE + local.start, piece * PIECE + local.stop)
-            nc.vector.scalar_tensor_tensor(
-                scaled[piece][:, local], y[:, local], b2_sb[:], routing[:, columns], ADD, MULT
-            )
-            queue.dma_start(out[:, columns], scaled[piece][:, local])
+            y = y_bank[piece][:, local]
+            scaled = work.tile([P, HALF], F32, name="scaled", bufs=2 * PIECES)
+            if by_gpsimd:
+                shifted = work.tile([P, HALF], F32, name="shifted", bufs=1)
+                nc.scalar.activation(shifted[:], y, IDENTITY, bias=b2_sb[:])
+                nc.gpsimd.tensor_tensor(scaled[:], shifted[:], routing[:, columns], MULT)
+                nc.scalar.dma_start(out[:, columns], scaled[:])
+            else:
+                nc.vector.scalar_tensor_tensor(scaled[:], y, b2_sb[:], routing[:, columns], ADD, MULT)
+                nc.sync.dma_start(out[:, columns], scaled[:])
 
         for piece in range(last):
-            gather(lin_bank[piece], 1, piece, whole)
-            gather(gate_bank[piece], 0, piece, whole)
-        gather(lin_bank[last], 1, last, whole)
-        gather(last_gate_bank[0], 0, last, halves[0])
-        linear_half(0)
-        gather(last_gate_bank[1], 0, last, halves[1])
+            linear_half(piece)
+            gate_and_product(piece)
+        linear_half(last)
 
-        for piece in range(last):
-            gate_and_product(gate_bank[piece], piece, whole)
-            linear_half(piece + 1)
+        project(0)
+        scale_and_store(0, 0)
+        scale_and_store(0, 1)
+        gate_and_product(last)
 
-        gate_and_product(last_gate_bank[0], last, halves[0])
-        y = lin_bank[last]
-        for local in halves:
-            project(y, 0, local)
-        scale_and_store(y, 0, halves[0], nc.sync)
-        gate_and_product(last_gate_bank[1], last, halves[1])
-        scale_and_store(y, 0, halves[1], nc.sync)
-        y = last_gate_bank[0]
-        project(y, 1, whole)
-        columns = slice(PIECE, PIECE + PIECE // 2)
-        shifted = work.tile([P, PIECE // 2], F32, name="shifted")
-        nc.scalar.activation(shifted[:], y[:, halves[0]], IDENTITY, bias=b2_sb[:])
-        nc.gpsimd.tensor_tensor(scaled[1][:, halves[0]], shifted[:], routing[:, columns], MULT)
-        nc.scalar.dma_start(out[:, columns], scaled[1][:, halves[0]])
-        scale_and_store(y, 1, halves[1], nc.sync)
-        y = last_gate_bank[1]
-        project(y, 2, whole)
-        scale_and_store(y, 2, whole, nc.sync)
-        y = lin_bank[last - 1]
-        project(y, last, whole)
-        scale_and_store(y, last, halves[0], nc.sync)
-        scale_and_store(y, last, halves[1], nc.sync)
+        project(1)
+        scale_and_store(1, 0, by_gpsimd=True)
+        scale_and_store(1, 1)
+        for piece in range(2, PIECES):
+            project(piece)
+            scale_and_store(piece, 0)
+            scale_and_store(piece, 1)

@@ -62,10 +62,10 @@ def tile_moemlpfused_kernel(tc, x, w1, b1, w2, b2, ew, offs, out):
         h = [work.tile([P, PIECE], BF16, name="h") for _ in range(PIECES)]
         lin1 = [work.tile([P, PIECE], F32, name="lin1") for _ in range(PIECES)]
 
-        def linear_half(piece):
+        def linear_half(piece, clamp_engine):
             lin_raw = work.tile([P, PIECE], F32, name="lin_raw")
             nc.scalar.activation(lin_raw[:], lin_bank[piece][:], IDENTITY, bias=b1_lin1[:])
-            nc.vector.tensor_scalar(
+            clamp_engine.tensor_scalar(
                 lin1[piece][:], lin_raw[:], LIMIT + 1.0, -LIMIT + 1.0, MIN, MAX
             )
 
@@ -99,18 +99,17 @@ def tile_moemlpfused_kernel(tc, x, w1, b1, w2, b2, ew, offs, out):
                 nc.sync.dma_start(out[:, columns], scaled[:])
 
         for piece in range(last):
-            linear_half(piece)
+            linear_half(piece, nc.vector)
             gate_and_product(piece)
-        linear_half(last)
-
+        linear_half(last, nc.gpsimd)
         project(0)
         scale_and_store(0, 0)
         scale_and_store(0, 1)
+        project(1)
+        scale_and_store(1, 1)
         gate_and_product(last)
 
-        project(1)
         scale_and_store(1, 0, by_gpsimd=True)
-        scale_and_store(1, 1)
         for piece in range(2, PIECES):
             project(piece)
             scale_and_store(piece, 0)

@@ -22,7 +22,7 @@ def tile_moemlpfused_kernel(tc, x, w1, b1, w2, b2, ew, offs, out):
     nc = tc.nc
     with (
         tc.tile_pool(name="held", bufs=1) as held,
-        tc.tile_pool(name="work", bufs=PIECES) as work,
+        tc.tile_pool(name="work", bufs=PIECES + 1) as work,
         tc.psum_pool(name="psum", bufs=1) as psum,
     ):
         offsets = held.tile([P, ROUTED // 16], U16, name="offsets")
@@ -50,42 +50,49 @@ def tile_moemlpfused_kernel(tc, x, w1, b1, w2, b2, ew, offs, out):
 
         nc.vector.tensor_scalar_add(b1_lin1[:], b1_sb[:, 1:2], 1.0)
 
-        lin_bank = [banks[2 * piece] for piece in range(PIECES)]
-        gate_bank = [banks[2 * piece + 1] for piece in range(PIECES)]
-        for piece in range(PIECES):
-            picked = tokens[:].indirect(
-                offsets[:, piece * OFFSET_COLUMNS : (piece + 1) * OFFSET_COLUMNS]
-            )
-            nc.tensor.matmul(lin_bank[piece][:], w1_sb[:, P : 2 * P], picked)
-            nc.tensor.matmul(gate_bank[piece][:], w1_sb[:, 0:P], picked)
+        HALF = PIECE // 2
+        first_half, second_half, whole = slice(0, HALF), slice(HALF, PIECE), slice(0, PIECE)
+        units = [(0, first_half), (0, second_half)] + [(piece, whole) for piece in range(1, PIECES)]
+        lin_bank = [banks[(2 * unit) % PSUM_BANKS] for unit in range(len(units))]
+        gate_bank = [banks[(2 * unit + 1) % PSUM_BANKS] for unit in range(len(units))]
 
         h = [work.tile([P, PIECE], BF16, name="h") for _ in range(PIECES)]
         lin1 = [work.tile([P, PIECE], F32, name="lin1") for _ in range(PIECES)]
 
-        def linear_half(piece, clamp_engine):
+        def gather(unit):
+            piece, local = units[unit]
+            first = piece * OFFSET_COLUMNS
+            picked = tokens[:].indirect(offsets[:, first + local.start // 16 : first + local.stop // 16])
+            nc.tensor.matmul(lin_bank[unit][:, local], w1_sb[:, P : 2 * P], picked)
+            nc.tensor.matmul(gate_bank[unit][:, local], w1_sb[:, 0:P], picked)
+
+        def linear_half(unit, clamp_engine):
+            piece, local = units[unit]
             lin_raw = work.tile([P, PIECE], F32, name="lin_raw")
-            nc.scalar.activation(lin_raw[:], lin_bank[piece][:], IDENTITY, bias=b1_lin1[:])
+            nc.scalar.activation(
+                lin_raw[:, local], lin_bank[unit][:, local], IDENTITY, bias=b1_lin1[:]
+            )
             clamp_engine.tensor_scalar(
-                lin1[piece][:], lin_raw[:], LIMIT + 1.0, -LIMIT + 1.0, MIN, MAX
+                lin1[piece][:, local], lin_raw[:, local], LIMIT + 1.0, -LIMIT + 1.0, MIN, MAX
             )
 
-        def gate_and_product(piece):
+        def gate_and_product(unit):
+            piece, local = units[unit]
             swish = work.tile([P, PIECE], F32, name="swish")
-            nc.scalar.activation(swish[:], gate_bank[piece][:], SWISH, bias=b1_sb[:, 0:1])
+            nc.scalar.activation(
+                swish[:, local], gate_bank[unit][:, local], SWISH, bias=b1_sb[:, 0:1]
+            )
             nc.vector.scalar_tensor_tensor(
-                h[piece][:], swish[:], swish_cap[:], lin1[piece][:], MIN, MULT
+                h[piece][:, local], swish[:, local], swish_cap[:], lin1[piece][:, local], MIN, MULT
             )
 
-        last = PIECES - 1
+        last = len(units) - 1
         y_bank = [gate_bank[last - 1], lin_bank[last], gate_bank[last], lin_bank[last - 1]]
 
         def project(piece):
             nc.tensor.matmul(y_bank[piece][:], w2_sb[:], h[piece][:])
 
-        HALF = PIECE // 2
-
-        def scale_and_store(piece, half, by_gpsimd=False):
-            local = slice(half * HALF, (half + 1) * HALF)
+        def scale_and_store(piece, local, by_gpsimd=False):
             columns = slice(piece * PIECE + local.start, piece * PIECE + local.stop)
             y = y_bank[piece][:, local]
             scaled = work.tile([P, HALF], F32, name="scaled", bufs=2 * PIECES)
@@ -98,19 +105,26 @@ def tile_moemlpfused_kernel(tc, x, w1, b1, w2, b2, ew, offs, out):
                 nc.vector.scalar_tensor_tensor(scaled[:], y, b2_sb[:], routing[:, columns], ADD, MULT)
                 nc.sync.dma_start(out[:, columns], scaled[:])
 
-        for piece in range(last):
-            linear_half(piece, nc.vector)
-            gate_and_product(piece)
+        for unit in range(last):
+            gather(unit)
+        linear_half(0, nc.vector)
+        gate_and_product(0)
+        gather(last)
+        for unit in range(1, last):
+            linear_half(unit, nc.vector)
+            gate_and_product(unit)
         linear_half(last, nc.gpsimd)
         project(0)
-        scale_and_store(0, 0)
-        scale_and_store(0, 1)
+        scale_and_store(0, first_half)
+        scale_and_store(0, second_half)
         project(1)
-        scale_and_store(1, 1)
+        scale_and_store(1, first_half)
         gate_and_product(last)
+        scale_and_store(1, second_half)
 
-        scale_and_store(1, 0, by_gpsimd=True)
-        for piece in range(2, PIECES):
-            project(piece)
-            scale_and_store(piece, 0)
-            scale_and_store(piece, 1)
+        project(2)
+        scale_and_store(2, first_half, by_gpsimd=True)
+        scale_and_store(2, second_half)
+        project(3)
+        scale_and_store(3, first_half)
+        scale_and_store(3, second_half)

import concourse.mybir as mybir

P = 128
TOKENS = 4096
ROUTED = 2048
PIECE = 512
PIECES = ROUTED // PIECE
OFFSET_COLUMNS = PIECE // 16
PSUM_BANKS = 8
LIMIT = 7.0

FLOPS = 2 * P * (2 * P) * ROUTED + 2 * P * P * ROUTED

BF16, F32, U16 = mybir.dt.bfloat16, mybir.dt.float32, mybir.dt.uint16
ADD, MULT = mybir.AluOpType.add, mybir.AluOpType.mult
MIN, MAX = mybir.AluOpType.min, mybir.AluOpType.max
SWISH = mybir.ActivationFunctionType.Gelu_apprx_sigmoid
IDENTITY = mybir.ActivationFunctionType.Identity


def tile_moemlpfused_kernel(tc, x, w1, b1, w2, b2, ew, offs, out):
    nc = tc.nc
    with (
        tc.tile_pool(name="held", bufs=1) as held,
        tc.tile_pool(name="work", bufs=PIECES + 1) as work,
        tc.psum_pool(name="psum", bufs=1) as psum,
    ):
        offsets = held.tile([P, ROUTED // 16], U16, name="offsets")
        tokens = held.tile([P, TOKENS], BF16, name="tokens")
        w1_sb = held.tile([P, 2 * P], BF16, name="w1_sb")
        w2_sb = held.tile([P, P], BF16, name="w2_sb")
        b1_sb = held.tile([P, 2], F32, name="b1_sb")
        b1_lin1 = held.tile([P, 1], F32, name="b1_lin1")
        b2_sb = held.tile([P, 1], F32, name="b2_sb")
        routing = held.tile([P, ROUTED], F32, name="routing")
        limit = held.tile([P, 1], F32, name="limit")
        swish_cap = held.tile([P, 1], F32, name="swish_cap")
        banks = [psum.tile([P, PIECE], F32, name=f"bank{b}") for b in range(PSUM_BANKS)]

        nc.scalar.dma_start(tokens[:], x)
        nc.sync.dma_start(offsets[:], offs)
        nc.sync.dma_start(w1_sb[:], w1)
        nc.scalar.dma_start(b1_sb[:], b1.rearrange("(half p) one -> p (half one)", p=P))
        nc.scalar.dma_start(w2_sb[:], w2)
        nc.scalar.dma_start(b2_sb[:], b2)
        nc.scalar.dma_start(routing[:], ew.broadcast_to([P, ROUTED]))

        nc.vector.memset(limit[:], LIMIT)
        nc.scalar.activation(swish_cap[:], limit[:], SWISH)

        nc.vector.tensor_scalar_add(b1_lin1[:], b1_sb[:, 1:2], 1.0)

        HALF = PIECE // 2
        first_half, second_half, whole = slice(0, HALF), slice(HALF, PIECE), slice(0, PIECE)
        units = [(0, first_half), (0, second_half)] + [(piece, whole) for piece in range(1, PIECES)]
        lin_bank = [banks[(2 * unit) % PSUM_BANKS] for unit in range(len(units))]
        gate_bank = [banks[(2 * unit + 1) % PSUM_BANKS] for unit in range(len(units))]

        h = [work.tile([P, PIECE], BF16, name="h") for _ in range(PIECES)]
        lin1 = [work.tile([P, PIECE], F32, name="lin1") for _ in range(PIECES)]

        def gather(unit):
            piece, local = units[unit]
            first = piece * OFFSET_COLUMNS
            picked = tokens[:].indirect(offsets[:, first + local.start // 16 : first + local.stop // 16])
            nc.tensor.matmul(lin_bank[unit][:, local], w1_sb[:, P : 2 * P], picked)
            nc.tensor.matmul(gate_bank[unit][:, local], w1_sb[:, 0:P], picked)

        def linear_half(unit, clamp_engine):
            piece, local = units[unit]
            lin_raw = work.tile([P, PIECE], F32, name="lin_raw")
            nc.scalar.activation(
                lin_raw[:, local], lin_bank[unit][:, local], IDENTITY, bias=b1_lin1[:]
            )
            clamp_engine.tensor_scalar(
                lin1[piece][:, local], lin_raw[:, local], LIMIT + 1.0, -LIMIT + 1.0, MIN, MAX
            )

        def gate_and_product(unit):
            piece, local = units[unit]
            swish = work.tile([P, PIECE], F32, name="swish")
            nc.scalar.activation(
                swish[:, local], gate_bank[unit][:, local], SWISH, bias=b1_sb[:, 0:1]
            )
            nc.vector.scalar_tensor_tensor(
                h[piece][:, local], swish[:, local], swish_cap[:], lin1[piece][:, local], MIN, MULT
            )

        last = len(units) - 1
        y_bank = [gate_bank[last - 1], lin_bank[last], gate_bank[last], lin_bank[last - 1]]

        def project(piece):
            nc.tensor.matmul(y_bank[piece][:], w2_sb[:], h[piece][:])

        def scale_and_store(piece, local, by_gpsimd=False):
            columns = slice(piece * PIECE + local.start, piece * PIECE + local.stop)
            y = y_bank[piece][:, local]
            scaled = work.tile([P, HALF], F32, name="scaled", bufs=2 * PIECES)
            if by_gpsimd:
                shifted = work.tile([P, HALF], F32, name="shifted", bufs=1)
                nc.scalar.activation(shifted[:], y, IDENTITY, bias=b2_sb[:])
                nc.gpsimd.tensor_tensor(scaled[:], shifted[:], routing[:, columns], MULT)
                nc.scalar.dma_start(out[:, columns], scaled[:])
            else:
                nc.vector.scalar_tensor_tensor(scaled[:], y, b2_sb[:], routing[:, columns], ADD, MULT)
                nc.sync.dma_start(out[:, columns], scaled[:])

        for unit in range(last):
            gather(unit)
        linear_half(0, nc.vector)
        gate_and_product(0)
        gather(last)
        for unit in range(1, last):
            linear_half(unit, nc.vector)
            gate_and_product(unit)
        linear_half(last, nc.gpsimd)
        project(0)
        scale_and_store(0, first_half)
        scale_and_store(0, second_half)
        project(1)
        scale_and_store(1, first_half)
        gate_and_product(last)
        scale_and_store(1, second_half)

        project(2)
        scale_and_store(2, first_half, by_gpsimd=True)
        scale_and_store(2, second_half)
        project(3)
        scale_and_store(3, first_half)
        scale_and_store(3, second_half)
